import numpy as np
import ml_dtypes


def mxq(x, axis, fmt="e4m3"):
    dtype, down = {"e4m3": (ml_dtypes.float8_e4m3fn, 7), "e5m2": (ml_dtypes.float8_e5m2, 14)}[fmt]
    v = np.moveaxis(np.asarray(x, np.float32).astype(ml_dtypes.bfloat16).astype(np.float64), axis, -1)
    blocks = v.reshape(v.shape[:-1] + (-1, 32))
    amax = np.abs(blocks).max(-1, keepdims=True)
    byte = np.maximum(np.where(amax > 0, np.frexp(amax)[1] - 1 + 127, 0) - down, 1)
    scale = np.exp2(byte - 127.0)
    codes = (blocks / scale).astype(np.float32).astype(dtype).astype(np.float64)
    return np.moveaxis((codes * scale).reshape(v.shape), -1, axis)


WIDE = False


def mx_kscale(k):
    if not WIDE:
        return np.ones(k)
    levels = np.array([10, -10, 5, -5, 0])
    a = np.random.permutation(np.resize(levels, k // 512 * 4)).reshape(k // 512, 4)
    idx = np.arange(k)
    return np.exp2(a[idx // 512, idx % 128 // 32])


BF16 = ml_dtypes.bfloat16


def bf(x):
    return np.asarray(x, np.float32).astype(BF16)


def f64(x):
    return np.asarray(x).astype(np.float64)


E2M1 = np.array([0.0, 0.5, 1.0, 1.5, 2.0, 3.0, 4.0, 6.0, -0.0, -0.5, -1.0, -1.5, -2.0, -3.0, -4.0, -6.0])


def pack_weight(w, fmt):
    k, n = w.shape
    w = f64(bf(w)).reshape(k // 32, 32, n)
    amax = np.abs(w).max(1)
    if fmt == "e4m3":
        byte = np.frexp(amax)[1] - 1 + 127 - 7
    else:
        mant, ex = np.frexp(amax / 6.0)
        byte = np.where(mant > 0.5, ex, ex - 1) + 127
    byte = np.clip(np.where(amax > 0, byte, 1), 1, 254)
    scaled = (w * np.exp2(127.0 - byte)[:, None, :]).reshape(k, n).astype(np.float32)
    by_word = np.ascontiguousarray(scaled.reshape(k // 512, 128, 4, n).transpose(0, 1, 3, 2))
    if fmt == "e4m3":
        words = by_word.astype(ml_dtypes.float8_e4m3fn).view(np.uint8)
    else:
        c = by_word.astype(ml_dtypes.float4_e2m1fn).view(np.uint8) & 0xF
        words = c[..., 0::2] | (c[..., 1::2] << 4)
    return np.ascontiguousarray(words), np.ascontiguousarray(byte.astype(np.uint8).reshape(k // 512, 16, n))


def unpack_weight(words, scales, fmt):
    g, p, n, _ = words.shape
    if fmt == "e4m3":
        vals = np.ascontiguousarray(words).view(ml_dtypes.float8_e4m3fn).astype(np.float64)
    else:
        nib = np.empty((g, p, n, 4), np.uint8)
        nib[..., 0::2] = words & 0xF
        nib[..., 1::2] = words >> 4
        vals = E2M1[nib]
    vals = vals * np.repeat(np.exp2(scales.astype(np.float64) - 127.0), 8, axis=1)[..., None]
    return vals.transpose(0, 1, 3, 2).reshape(g * 512, n)


B, N, D = 1, 2048, 512
P = 0.125
C = np.sqrt(4.0 / (3.0 * P * N))


def erf(v):
    u = np.clip(v, -6.0, 6.0)
    t = u.copy()
    acc = u.copy()
    for n in range(1, 121):
        t = t * (2.0 * u * u / (2.0 * n + 1.0))
        acc = acc + t
    return 2.0 / np.sqrt(np.pi) * np.exp(-u * u) * acc


def gelu(v):
    return 0.5 * v * (1.0 + erf(v / np.sqrt(2.0)))


def draw_adj():
    a = np.random.random((B, N, N)) * (np.random.random((B, N, N)) < P)
    return a * (np.random.random((B, N, 1)) > 0.05)


def setup_inputs():
    s = mx_kscale(D)
    x = bf(np.random.standard_normal((B, N, D)) * s)
    mask = bf(np.random.random((B, N)) > 0.2)
    adj = bf(draw_adj())
    w0 = np.random.standard_normal((D, D)) * 0.7 / (C * np.sqrt(D)) / s
    words, scales = pack_weight(w0.T, "e4m3")
    b0 = bf(np.random.standard_normal(D) * 0.3)
    return {"x": x,
            "mask": mask,
            "adj": adj,
            "W0_words": words,
            "W0_scales": scales,
            "b0": b0}


def reference(x, mask, adj, W0_words, W0_scales, b0):
    a = f64(adj)
    deg = a.sum(-1)
    dinv = np.where(deg != 0, 1.0 / np.where(deg != 0, deg, 1.0), 0.0)
    adj_n = a * dinv[..., None]
    h = (mxq(f64(x), 2, "e4m3") @ unpack_weight(W0_words, W0_scales, "e4m3")) + f64(b0)
    z = mxq(adj_n, 2, "e4m3") @ mxq(h, 1, "e4m3")
    return gelu(z * f64(mask)[..., None])

@@ -1,0 +1,282 @@
+from contextlib import ExitStack
+
+import concourse.mybir as mybir
+from concourse.masks import make_identity
+
+F32 = mybir.dt.float32
+BF16 = mybir.dt.bfloat16
+I32 = mybir.dt.int32
+U32 = mybir.dt.uint32
+U8 = mybir.dt.uint8
+FP8X4 = mybir.dt.float8_e4m3fn_x4
+ALU = mybir.AluOpType
+ACT = mybir.ActivationFunctionType
+
+P = 128
+PACK = 4
+K_PASS = P * PACK
+NODES = 2048
+FEAT = 512
+PASSES = NODES // K_PASS
+ROW_TILES = NODES // P
+CHUNK = 2
+CHUNKS = ROW_TILES // CHUNK
+WORDS = NODES // 2
+VECTOR_SUM_COLS = 1280
+SUM_AHEAD = 3
+
+FLOPS = 2 * NODES * FEAT * FEAT + 2 * NODES * NODES * FEAT
+
+
+def tile_graphconvlayer_pa_kernel(tc, x, mask, adj, W0_words, W0_scales, b0, out):
+    nc = tc.nc
+    with ExitStack() as stack:
+        keep = stack.enter_context(tc.tile_pool(name="keep", bufs=1))
+        stage2 = stack.enter_context(tc.tile_pool(name="stage2", bufs=2))
+        stage4 = stack.enter_context(tc.tile_pool(name="stage4", bufs=4))
+        turned = stack.enter_context(tc.psum_pool(name="turned", bufs=4))
+        sums = stack.enter_context(tc.psum_pool(name="sums", bufs=4))
+
+        ident = keep.tile([P, P], F32)
+        make_identity(nc, ident[:])
+        ones = keep.tile([P, P], BF16)
+        nc.vector.memset(ones[:], 1.0)
+        rows = keep.tile([P, FEAT + P], BF16)
+        nc.vector.memset(rows[:], 0.0)
+        w_scales = keep.tile([P, FEAT], U8, align_bytes=64)
+        nc.vector.memset(w_scales[:].bitcast(I32), 0)
+        cold = keep.tile([P, 1], F32)
+        nc.vector.memset(cold[:], 0.0)
+        warm = keep.tile([P, 1], F32)
+        nc.scalar.activation(out=warm[:], in_=cold[:], func=ACT.Gelu)
+
+        x_raw = [keep.tile([P, 2, 2 * FEAT], BF16, name="x_raw%d" % g) for g in range(PASSES)]
+        adj_raw = [keep.tile([P, CHUNK, NODES], BF16, name="adj_raw%d" % c) for c in range(CHUNKS)]
+        w_codes = keep.tile([P, FEAT], U32, align_bytes=64)
+
+        def load_x(g):
+            nc.sync.dma_start(
+                out=x_raw[g][:],
+                in_=x[0, K_PASS * g : K_PASS * (g + 1), :].rearrange("(u j e) k -> j u (e k)", u=2, e=2),
+            )
+
+        load_x(0)
+        nc.sync.dma_start(
+            out=w_codes[:].bitcast(I32),
+            in_=W0_words[0].rearrange("p n t -> p (n t)").bitcast(I32),
+        )
+        for quadrant in range(4):
+            nc.sync.dma_start(
+                out=w_scales[32 * quadrant : 32 * quadrant + 4, :].bitcast(I32),
+                in_=W0_scales[0, 4 * quadrant : 4 * quadrant + 4, :].bitcast(I32),
+            )
+        nc.scalar.dma_start(out=rows[0:1, 0:FEAT], in_=b0.rearrange("(o f) -> o f", o=1))
+        nc.scalar.dma_start(out=rows[0:ROW_TILES, FEAT:], in_=mask[0].rearrange("(i p) -> i p", p=P))
+        for g in range(1, PASSES):
+            load_x(g)
+        for c in range(CHUNKS):
+            nc.sync.dma_start(
+                out=adj_raw[c][:],
+                in_=adj[0, CHUNK * P * c : CHUNK * P * (c + 1), :].rearrange("(j p) m -> p j m", p=P),
+            )
+
+        bias_ps = sums.tile([P, FEAT], F32, tag="sums")
+        nc.tensor.matmul(out=bias_ps[:], lhsT=ones[:], rhs=rows[:, 0:FEAT], start=True, stop=True)
+        bias = keep.tile([P, FEAT], F32)
+        nc.vector.tensor_copy(out=bias[:], in_=bias_ps[:])
+        mask_rows = keep.tile([P, P], F32)
+        nc.vector.tensor_copy(out=mask_rows[:], in_=rows[:, FEAT:])
+        mask_ps = turned.tile([P, P], F32, tag="turned")
+        nc.tensor.transpose(out=mask_ps[:], in_=mask_rows[:], identity=ident[:])
+        mask_col = keep.tile([P, ROW_TILES], F32)
+        nc.vector.tensor_copy(out=mask_col[:], in_=mask_ps[:, 0:ROW_TILES])
+
+        x_codes = [keep.tile([P, K_PASS], U32, name="x_codes%d" % g, align_bytes=64) for g in range(PASSES)]
+        x_scales = [keep.tile([P, K_PASS], U8, name="x_scales%d" % g, align_bytes=64) for g in range(PASSES)]
+        h_codes = [keep.tile([P, FEAT], U32, name="h_codes%d" % g, align_bytes=64) for g in range(PASSES)]
+        h_scales = [keep.tile([P, FEAT], U8, name="h_scales%d" % g, align_bytes=64) for g in range(PASSES)]
+        x_grouped = {}
+
+        def turn_x(g):
+            x_grouped[g] = stage2.tile([P, PACK * K_PASS], BF16, name="x_grouped", align_bytes=64)
+            grouped_words = x_grouped[g][:].bitcast(F32).rearrange("p (t j v) -> p t j v", t=PACK, v=2)
+            for u in range(2):
+                x_turned = turned.tile([P, 2, 2, P], F32, tag="turned")
+                for e in range(2):
+                    words = x_raw[g][:, u, FEAT * e : FEAT * (e + 1)].bitcast(F32)
+                    for v in range(2):
+                        nc.tensor.transpose(
+                            out=x_turned[:, e, v, :], in_=words[:, v : FEAT // 2 : 2], identity=ident[:]
+                        )
+                nc.scalar.copy(
+                    out=grouped_words[:, 2 * u : 2 * u + 2, :, :],
+                    in_=x_turned[:].rearrange("p e v j -> p e j v"),
+                )
+
+        def quantise_x(g):
+            nc.vector.quantize_mx(out=x_codes[g][:].bitcast(FP8X4), scales=x_scales[g][:], in_=x_grouped[g][:])
+
+        def make_h(g):
+            h_grouped = stage2.tile([P, PACK * FEAT], BF16, name="h_grouped", align_bytes=64)
+            grouped = h_grouped[:].rearrange("p (f t) -> p f t", t=PACK)
+            for block in range(FEAT // P):
+                f_cols = slice(P * block, P * (block + 1))
+                h_ps = sums.tile([P, PACK, P], F32, tag="sums")
+                for t in range(PACK):
+                    node_cols = slice(P * t, P * (t + 1))
+                    nc.tensor.matmul_mx(
+                        out=h_ps[:, t, :],
+                        lhsT=x_codes[g][:, node_cols].bitcast(FP8X4),
+                        lhsT_scale=x_scales[g][:, node_cols],
+                        rhs=w_codes[:, f_cols].bitcast(FP8X4),
+                        rhs_scale=w_scales[:, f_cols],
+                        start=True,
+                        stop=True,
+                    )
+                nc.vector.tensor_tensor(
+                    out=grouped[:, f_cols, :],
+                    in0=h_ps[:].rearrange("p t f -> p f t"),
+                    in1=bias[:, f_cols].unsqueeze(2).to_broadcast([P, P, PACK]),
+                    op=ALU.add,
+                )
+            nc.vector.quantize_mx(out=h_codes[g][:].bitcast(FP8X4), scales=h_scales[g][:], in_=h_grouped[:])
+
+        adj_codes = [keep.tile([P, K_PASS], U32, name="adj_codes%d" % i, align_bytes=64) for i in range(ROW_TILES)]
+        adj_scales = [keep.tile([P, K_PASS], U8, name="adj_scales%d" % i, align_bytes=64) for i in range(ROW_TILES)]
+        vector_sum = {}
+        scalar_sum = {}
+        adj_n = {}
+        adj_turned = {}
+        adj_grouped = {}
+        z_ps = {}
+
+        def sum_rows_scalar(c):
+            scalar_sum[c] = stage4.tile([P, CHUNK], F32, name="scalar_sum")
+            for j in range(CHUNK):
+                unread = stage2.tile([P, NODES - VECTOR_SUM_COLS], BF16, name="unread_scalar")
+                nc.scalar.activation(
+                    out=unread[:],
+                    in_=adj_raw[c][:, j, VECTOR_SUM_COLS:],
+                    func=ACT.Copy,
+                    accum_out=scalar_sum[c][:, j : j + 1],
+                )
+
+        def sum_rows_vector(c):
+            vector_sum[c] = stage4.tile([P, CHUNK], F32, name="vector_sum")
+            for j in range(CHUNK):
+                unread = stage2.tile([P, VECTOR_SUM_COLS], BF16, name="unread_vector")
+                nc.vector.tensor_scalar(
+                    out=unread[:],
+                    in0=adj_raw[c][:, j, 0:VECTOR_SUM_COLS],
+                    scalar1=1.0,
+                    scalar2=None,
+                    op0=ALU.mult,
+                    op1=ALU.add,
+                    accum_out=vector_sum[c][:, j : j + 1],
+                )
+
+        def normalise(c):
+            deg = stage4.tile([P, CHUNK], F32, name="deg")
+            nc.vector.tensor_tensor(out=deg[:], in0=vector_sum[c][:], in1=scalar_sum[c][:], op=ALU.add)
+            divisor = stage4.tile([P, CHUNK], F32, name="divisor")
+            nc.vector.scalar_tensor_tensor(
+                out=divisor[:], in0=deg[:], scalar=0.0, in1=deg[:], op0=ALU.is_equal, op1=ALU.add
+            )
+            inverse = stage4.tile([P, CHUNK], F32, name="inverse")
+            nc.vector.reciprocal(out=inverse[:], in_=divisor[:])
+            dinv = stage4.tile([P, CHUNK], F32, name="dinv")
+            nc.vector.scalar_tensor_tensor(
+                out=dinv[:], in0=deg[:], scalar=0.0, in1=inverse[:], op0=ALU.not_equal, op1=ALU.mult
+            )
+            for j in range(CHUNK):
+                adj_n[c, j] = stage4.tile([P, NODES], BF16, name="adj_n")
+                nc.vector.tensor_scalar(
+                    out=adj_n[c, j][:],
+                    in0=adj_raw[c][:, j, :],
+                    scalar1=dinv[:, j : j + 1],
+                    scalar2=None,
+                    op0=ALU.mult,
+                )
+
+        def turn_adj(c):
+            for j in range(CHUNK):
+                words = adj_n[c, j][:].bitcast(F32)
+                for half in range(PASSES // 2):
+                    bank = turned.tile([P, 2, 2, P], F32, tag="turned")
+                    adj_turned[c, j, half] = bank
+                    for g2 in range(2):
+                        for u in range(2):
+                            first = P * (2 * (2 * half + g2) + u)
+                            nc.tensor.transpose(
+                                out=bank[:, g2, u, :], in_=words[:, first : first + P], identity=ident[:]
+                            )
+
+        def regroup_adj(c):
+            for j in range(CHUNK):
+                adj_grouped[c, j] = stage4.tile([P, PACK * K_PASS], BF16, name="adj_grouped", align_bytes=64)
+                grouped_words = adj_grouped[c, j][:].bitcast(F32).rearrange("p (g n u) -> p g n u", g=PASSES, u=2)
+                for half in range(PASSES // 2):
+                    nc.scalar.copy(
+                        out=grouped_words[:, 2 * half : 2 * half + 2, :, :],
+                        in_=adj_turned[c, j, half][:].rearrange("p g u n -> p g n u"),
+                    )
+
+        def quantise_adj(c):
+            for j in range(CHUNK):
+                i = CHUNK * c + j
+                nc.vector.quantize_mx(
+                    out=adj_codes[i][:].bitcast(FP8X4), scales=adj_scales[i][:], in_=adj_grouped[c, j][:]
+                )
+
+        def aggregate(c):
+            for j in range(CHUNK):
+                i = CHUNK * c + j
+                z_ps[i] = sums.tile([P, FEAT], F32, name="z_ps", tag="sums")
+                for g in range(PASSES):
+                    row_cols = slice(P * g, P * (g + 1))
+                    nc.tensor.matmul_mx(
+                        out=z_ps[i][:],
+                        lhsT=adj_codes[i][:, row_cols].bitcast(FP8X4),
+                        lhsT_scale=adj_scales[i][:, row_cols],
+                        rhs=h_codes[g][:].bitcast(FP8X4),
+                        rhs_scale=h_scales[g][:],
+                        start=(g == 0),
+                        stop=(g == PASSES - 1),
+                    )
+
+        def finish(c):
+            for j in range(CHUNK):
+                i = CHUNK * c + j
+                result = stage4.tile([P, FEAT], F32, name="result")
+                nc.scalar.activation(out=result[:], in_=z_ps[i][:], func=ACT.Gelu, scale=mask_col[:, i : i + 1])
+                nc.sync.dma_start(out=out[0, P * i : P * (i + 1), :], in_=result[:])
+
+        def in_range(c):
+            return 0 <= c < CHUNKS
+
+        turn_x(0)
+        quantise_x(0)
+        for r in range(-PASSES, CHUNKS + 1):
+            g = r + PASSES
+            if in_range(r - 1):
+                quantise_adj(r - 1)
+            if in_range(r):
+                turn_adj(r)
+            if in_range(r - 1):
+                aggregate(r - 1)
+            if g + 1 < PASSES:
+                turn_x(g + 1)
+            if in_range(r + SUM_AHEAD):
+                sum_rows_scalar(r + SUM_AHEAD)
+            if in_range(r):
+                regroup_adj(r)
+            if in_range(r - 1):
+                finish(r - 1)
+            if g + 1 < PASSES:
+                quantise_x(g + 1)
+            if g < PASSES:
+                make_h(g)
+            if in_range(r + SUM_AHEAD):
+                sum_rows_vector(r + SUM_AHEAD)
+            if in_range(r + 1):
+                normalise(r + 1)

@@ -36,13 +36,16 @@ def tile_graphconvlayer_pa_kernel(tc, x, mask, adj, W0_words, W0_scales, b0, out
         stage4 = stack.enter_context(tc.tile_pool(name="stage4", bufs=4))
         turned = stack.enter_context(tc.psum_pool(name="turned", bufs=4))
         sums = stack.enter_context(tc.psum_pool(name="sums", bufs=4))
+        stack.enter_context(tc.manual_schedule())
 
         ident = keep.tile([P, P], F32)
         make_identity(nc, ident[:])
-        ones = keep.tile([P, P], BF16)
-        nc.vector.memset(ones[:], 1.0)
         rows = keep.tile([P, FEAT + P], BF16)
         nc.vector.memset(rows[:], 0.0)
+        nc.scalar.dma_start(out=rows[0:1, 0:FEAT], in_=b0.rearrange("(o f) -> o f", o=1))
+        nc.scalar.dma_start(out=rows[0:ROW_TILES, FEAT:], in_=mask[0].rearrange("(i p) -> i p", p=P))
+        ones = keep.tile([P, P], BF16)
+        nc.vector.memset(ones[:], 1.0)
         w_scales = keep.tile([P, FEAT], U8, align_bytes=64)
         nc.vector.memset(w_scales[:].bitcast(I32), 0)
         cold = keep.tile([P, 1], F32)
@@ -70,8 +73,6 @@ def tile_graphconvlayer_pa_kernel(tc, x, mask, adj, W0_words, W0_scales, b0, out
                 out=w_scales[32 * quadrant : 32 * quadrant + 4, :].bitcast(I32),
                 in_=W0_scales[0, 4 * quadrant : 4 * quadrant + 4, :].bitcast(I32),
             )
-        nc.scalar.dma_start(out=rows[0:1, 0:FEAT], in_=b0.rearrange("(o f) -> o f", o=1))
-        nc.scalar.dma_start(out=rows[0:ROW_TILES, FEAT:], in_=mask[0].rearrange("(i p) -> i p", p=P))
         for g in range(1, PASSES):
             load_x(g)
         for c in range(CHUNKS):
@@ -80,16 +81,18 @@ def tile_graphconvlayer_pa_kernel(tc, x, mask, adj, W0_words, W0_scales, b0, out
                 in_=adj[0, CHUNK * P * c : CHUNK * P * (c + 1), :].rearrange("(j p) m -> p j m", p=P),
             )
 
-        bias_ps = sums.tile([P, FEAT], F32, tag="sums")
-        nc.tensor.matmul(out=bias_ps[:], lhsT=ones[:], rhs=rows[:, 0:FEAT], start=True, stop=True)
         bias = keep.tile([P, FEAT], F32)
-        nc.vector.tensor_copy(out=bias[:], in_=bias_ps[:])
-        mask_rows = keep.tile([P, P], F32)
-        nc.vector.tensor_copy(out=mask_rows[:], in_=rows[:, FEAT:])
-        mask_ps = turned.tile([P, P], F32, tag="turned")
-        nc.tensor.transpose(out=mask_ps[:], in_=mask_rows[:], identity=ident[:])
         mask_col = keep.tile([P, ROW_TILES], F32)
-        nc.vector.tensor_copy(out=mask_col[:], in_=mask_ps[:, 0:ROW_TILES])
+
+        def spread_bias_and_mask():
+            mask_rows = keep.tile([P, P], F32)
+            nc.vector.tensor_copy(out=mask_rows[:], in_=rows[:, FEAT:])
+            mask_ps = turned.tile([P, P], F32, tag="turned")
+            nc.tensor.transpose(out=mask_ps[:], in_=mask_rows[:], identity=ident[:])
+            bias_ps = sums.tile([P, FEAT], F32, tag="sums")
+            nc.tensor.matmul(out=bias_ps[:], lhsT=ones[:], rhs=rows[:, 0:FEAT], start=True, stop=True)
+            nc.vector.tensor_copy(out=mask_col[:], in_=mask_ps[:, 0:ROW_TILES])
+            nc.vector.tensor_copy(out=bias[:], in_=bias_ps[:])
 
         x_codes = [keep.tile([P, K_PASS], U32, name="x_codes%d" % g, align_bytes=64) for g in range(PASSES)]
         x_scales = [keep.tile([P, K_PASS], U8, name="x_scales%d" % g, align_bytes=64) for g in range(PASSES)]
@@ -255,6 +258,7 @@ def tile_graphconvlayer_pa_kernel(tc, x, mask, adj, W0_words, W0_scales, b0, out
             return 0 <= c < CHUNKS
 
         turn_x(0)
+        spread_bias_and_mask()
         quantise_x(0)
         for r in range(-PASSES, CHUNKS + 1):
             g = r + PASSES

@@ -22,8 +22,8 @@ ROW_TILES = NODES // P
 CHUNK = 2
 CHUNKS = ROW_TILES // CHUNK
 WORDS = NODES // 2
-VECTOR_SUM_COLS = 1280
-SUM_AHEAD = 3
+SCALAR_ONLY_CHUNKS = 2
+VECTOR_SUM_COLS = 1536
 
 FLOPS = 2 * NODES * FEAT * FEAT + 2 * NODES * NODES * FEAT
 
@@ -153,24 +153,27 @@ def tile_graphconvlayer_pa_kernel(tc, x, mask, adj, W0_words, W0_scales, b0, out
         adj_grouped = {}
         z_ps = {}
 
-        def sum_rows_scalar(c):
+        def vector_cols(c):
+            return 0 if c < SCALAR_ONLY_CHUNKS else VECTOR_SUM_COLS
+
+        def sum_rows(c):
             scalar_sum[c] = stage4.tile([P, CHUNK], F32, name="scalar_sum")
             for j in range(CHUNK):
-                unread = stage2.tile([P, NODES - VECTOR_SUM_COLS], BF16, name="unread_scalar")
+                unread = stage2.tile([P, NODES - vector_cols(c)], BF16, name="unread_scalar")
                 nc.scalar.activation(
                     out=unread[:],
-                    in_=adj_raw[c][:, j, VECTOR_SUM_COLS:],
+                    in_=adj_raw[c][:, j, vector_cols(c) :],
                     func=ACT.Copy,
                     accum_out=scalar_sum[c][:, j : j + 1],
                 )
-
-        def sum_rows_vector(c):
+            if vector_cols(c) == 0:
+                return
             vector_sum[c] = stage4.tile([P, CHUNK], F32, name="vector_sum")
             for j in range(CHUNK):
-                unread = stage2.tile([P, VECTOR_SUM_COLS], BF16, name="unread_vector")
+                unread = stage2.tile([P, vector_cols(c)], BF16, name="unread_vector")
                 nc.vector.tensor_scalar(
                     out=unread[:],
-                    in0=adj_raw[c][:, j, 0:VECTOR_SUM_COLS],
+                    in0=adj_raw[c][:, j, 0 : vector_cols(c)],
                     scalar1=1.0,
                     scalar2=None,
                     op0=ALU.mult,
@@ -179,8 +182,10 @@ def tile_graphconvlayer_pa_kernel(tc, x, mask, adj, W0_words, W0_scales, b0, out
                 )
 
         def normalise(c):
-            deg = stage4.tile([P, CHUNK], F32, name="deg")
-            nc.vector.tensor_tensor(out=deg[:], in0=vector_sum[c][:], in1=scalar_sum[c][:], op=ALU.add)
+            deg = scalar_sum[c]
+            if vector_cols(c) > 0:
+                deg = stage4.tile([P, CHUNK], F32, name="deg")
+                nc.vector.tensor_tensor(out=deg[:], in0=vector_sum[c][:], in1=scalar_sum[c][:], op=ALU.add)
             divisor = stage4.tile([P, CHUNK], F32, name="divisor")
             nc.vector.scalar_tensor_tensor(
                 out=divisor[:], in0=deg[:], scalar=0.0, in1=deg[:], op0=ALU.is_equal, op1=ALU.add
@@ -262,25 +267,22 @@ def tile_graphconvlayer_pa_kernel(tc, x, mask, adj, W0_words, W0_scales, b0, out
         quantise_x(0)
         for r in range(-PASSES, CHUNKS + 1):
             g = r + PASSES
-            if in_range(r - 1):
-                quantise_adj(r - 1)
-            if in_range(r):
-                turn_adj(r)
-            if in_range(r - 1):
-                aggregate(r - 1)
+            if in_range(r + 1):
+                normalise(r + 1)
             if g + 1 < PASSES:
                 turn_x(g + 1)
-            if in_range(r + SUM_AHEAD):
-                sum_rows_scalar(r + SUM_AHEAD)
-            if in_range(r):
-                regroup_adj(r)
-            if in_range(r - 1):
-                finish(r - 1)
-            if g + 1 < PASSES:
                 quantise_x(g + 1)
             if g < PASSES:
                 make_h(g)
-            if in_range(r + SUM_AHEAD):
-                sum_rows_vector(r + SUM_AHEAD)
+            if in_range(r - 1):
+                aggregate(r - 1)
             if in_range(r + 1):
-                normalise(r + 1)
+                turn_adj(r + 1)
+            if in_range(r + 2):
+                sum_rows(r + 2)
+            if in_range(r - 1):
+                finish(r - 1)
+            if in_range(r + 1):
+                regroup_adj(r + 1)
+            if in_range(r):
+                quantise_adj(r)

@@ -23,7 +23,7 @@ CHUNK = 2
 CHUNKS = ROW_TILES // CHUNK
 WORDS = NODES // 2
 SCALAR_ONLY_CHUNKS = 2
-VECTOR_SUM_COLS = 1536
+VECTOR_SUM_COLS = 1280
 
 FLOPS = 2 * NODES * FEAT * FEAT + 2 * NODES * NODES * FEAT
 

@@ -23,7 +23,8 @@ CHUNK = 2
 CHUNKS = ROW_TILES // CHUNK
 WORDS = NODES // 2
 SCALAR_ONLY_CHUNKS = 2
-VECTOR_SUM_COLS = 1280
+VECTOR_SUM_COLS = 1536
+H_LEAD = 9
 
 FLOPS = 2 * NODES * FEAT * FEAT + 2 * NODES * NODES * FEAT
 
@@ -119,35 +120,42 @@ def tile_graphconvlayer_pa_kernel(tc, x, mask, adj, W0_words, W0_scales, b0, out
         def quantise_x(g):
             nc.vector.quantize_mx(out=x_codes[g][:].bitcast(FP8X4), scales=x_scales[g][:], in_=x_grouped[g][:])
 
-        def make_h(g):
-            h_grouped = stage2.tile([P, PACK * FEAT], BF16, name="h_grouped", align_bytes=64)
-            grouped = h_grouped[:].rearrange("p (f t) -> p f t", t=PACK)
-            for block in range(FEAT // P):
-                f_cols = slice(P * block, P * (block + 1))
-                h_ps = sums.tile([P, PACK, P], F32, tag="sums")
-                for t in range(PACK):
-                    node_cols = slice(P * t, P * (t + 1))
-                    nc.tensor.matmul_mx(
-                        out=h_ps[:, t, :],
-                        lhsT=x_codes[g][:, node_cols].bitcast(FP8X4),
-                        lhsT_scale=x_scales[g][:, node_cols],
-                        rhs=w_codes[:, f_cols].bitcast(FP8X4),
-                        rhs_scale=w_scales[:, f_cols],
-                        start=True,
-                        stop=True,
-                    )
-                nc.vector.tensor_tensor(
-                    out=grouped[:, f_cols, :],
-                    in0=h_ps[:].rearrange("p t f -> p f t"),
-                    in1=bias[:, f_cols].unsqueeze(2).to_broadcast([P, P, PACK]),
-                    op=ALU.add,
+        h_grouped = {}
+
+        def make_h(g, block):
+            if block == 0:
+                h_grouped[g] = stage2.tile([P, PACK * FEAT], BF16, name="h_grouped", align_bytes=64)
+            f_cols = slice(P * block, P * (block + 1))
+            h_ps = sums.tile([P, PACK, P], F32, tag="sums")
+            for t in range(PACK):
+                node_cols = slice(P * t, P * (t + 1))
+                nc.tensor.matmul_mx(
+                    out=h_ps[:, t, :],
+                    lhsT=x_codes[g][:, node_cols].bitcast(FP8X4),
+                    lhsT_scale=x_scales[g][:, node_cols],
+                    rhs=w_codes[:, f_cols].bitcast(FP8X4),
+                    rhs_scale=w_scales[:, f_cols],
+                    start=True,
+                    stop=True,
                 )
-            nc.vector.quantize_mx(out=h_codes[g][:].bitcast(FP8X4), scales=h_scales[g][:], in_=h_grouped[:])
+            nc.vector.tensor_tensor(
+                out=h_grouped[g][:].rearrange("p (f t) -> p f t", t=PACK)[:, f_cols, :],
+                in0=h_ps[:].rearrange("p t f -> p f t"),
+                in1=bias[:, f_cols].unsqueeze(2).to_broadcast([P, P, PACK]),
+                op=ALU.add,
+            )
+
+        def quantise_h(g):
+            nc.vector.quantize_mx(out=h_codes[g][:].bitcast(FP8X4), scales=h_scales[g][:], in_=h_grouped[g][:])
 
         adj_codes = [keep.tile([P, K_PASS], U32, name="adj_codes%d" % i, align_bytes=64) for i in range(ROW_TILES)]
         adj_scales = [keep.tile([P, K_PASS], U8, name="adj_scales%d" % i, align_bytes=64) for i in range(ROW_TILES)]
         vector_sum = {}
         scalar_sum = {}
+        deg = {}
+        divisor = {}
+        inverse = {}
+        dinv = {}
         adj_n = {}
         adj_turned = {}
         adj_grouped = {}
@@ -156,133 +164,140 @@ def tile_graphconvlayer_pa_kernel(tc, x, mask, adj, W0_words, W0_scales, b0, out
         def vector_cols(c):
             return 0 if c < SCALAR_ONLY_CHUNKS else VECTOR_SUM_COLS
 
-        def sum_rows(c):
-            scalar_sum[c] = stage4.tile([P, CHUNK], F32, name="scalar_sum")
-            for j in range(CHUNK):
-                unread = stage2.tile([P, NODES - vector_cols(c)], BF16, name="unread_scalar")
-                nc.scalar.activation(
-                    out=unread[:],
-                    in_=adj_raw[c][:, j, vector_cols(c) :],
-                    func=ACT.Copy,
-                    accum_out=scalar_sum[c][:, j : j + 1],
-                )
+        def sum_rows_scalar(i):
+            c, j = divmod(i, CHUNK)
+            if j == 0:
+                scalar_sum[c] = stage4.tile([P, CHUNK], F32, name="scalar_sum")
+            unread = stage2.tile([P, NODES - vector_cols(c)], BF16, name="unread_scalar")
+            nc.scalar.activation(
+                out=unread[:],
+                in_=adj_raw[c][:, j, vector_cols(c) :],
+                func=ACT.Copy,
+                accum_out=scalar_sum[c][:, j : j + 1],
+            )
+
+        def sum_rows_vector(i):
+            c, j = divmod(i, CHUNK)
             if vector_cols(c) == 0:
                 return
-            vector_sum[c] = stage4.tile([P, CHUNK], F32, name="vector_sum")
-            for j in range(CHUNK):
-                unread = stage2.tile([P, vector_cols(c)], BF16, name="unread_vector")
-                nc.vector.tensor_scalar(
-                    out=unread[:],
-                    in0=adj_raw[c][:, j, 0 : vector_cols(c)],
-                    scalar1=1.0,
-                    scalar2=None,
-                    op0=ALU.mult,
-                    op1=ALU.add,
-                    accum_out=vector_sum[c][:, j : j + 1],
-                )
-
-        def normalise(c):
-            deg = scalar_sum[c]
-            if vector_cols(c) > 0:
-                deg = stage4.tile([P, CHUNK], F32, name="deg")
-                nc.vector.tensor_tensor(out=deg[:], in0=vector_sum[c][:], in1=scalar_sum[c][:], op=ALU.add)
-            divisor = stage4.tile([P, CHUNK], F32, name="divisor")
-            nc.vector.scalar_tensor_tensor(
-                out=divisor[:], in0=deg[:], scalar=0.0, in1=deg[:], op0=ALU.is_equal, op1=ALU.add
+            if j == 0:
+                vector_sum[c] = stage4.tile([P, CHUNK], F32, name="vector_sum")
+            unread = stage2.tile([P, vector_cols(c)], BF16, name="unread_vector")
+            nc.vector.tensor_scalar(
+                out=unread[:],
+                in0=adj_raw[c][:, j, 0 : vector_cols(c)],
+                scalar1=1.0,
+                scalar2=None,
+                op0=ALU.mult,
+                op1=ALU.add,
+                accum_out=vector_sum[c][:, j : j + 1],
             )
-            inverse = stage4.tile([P, CHUNK], F32, name="inverse")
-            nc.vector.reciprocal(out=inverse[:], in_=divisor[:])
-            dinv = stage4.tile([P, CHUNK], F32, name="dinv")
-            nc.vector.scalar_tensor_tensor(
-                out=dinv[:], in0=deg[:], scalar=0.0, in1=inverse[:], op0=ALU.not_equal, op1=ALU.mult
+
+        def invert_degree(c, step):
+            if step == 0:
+                deg[c] = scalar_sum[c]
+                if vector_cols(c) > 0:
+                    deg[c] = stage4.tile([P, CHUNK], F32, name="deg")
+                    nc.vector.tensor_tensor(out=deg[c][:], in0=vector_sum[c][:], in1=scalar_sum[c][:], op=ALU.add)
+            if step == 1:
+                divisor[c] = stage4.tile([P, CHUNK], F32, name="divisor")
+                nc.vector.scalar_tensor_tensor(
+                    out=divisor[c][:], in0=deg[c][:], scalar=0.0, in1=deg[c][:], op0=ALU.is_equal, op1=ALU.add
+                )
+            if step == 2:
+                inverse[c] = stage4.tile([P, CHUNK], F32, name="inverse")
+                nc.vector.reciprocal(out=inverse[c][:], in_=divisor[c][:])
+            if step == 3:
+                dinv[c] = stage4.tile([P, CHUNK], F32, name="dinv")
+                nc.vector.scalar_tensor_tensor(
+                    out=dinv[c][:], in0=deg[c][:], scalar=0.0, in1=inverse[c][:], op0=ALU.not_equal, op1=ALU.mult
+                )
+
+        def normalise(i):
+            c, j = divmod(i, CHUNK)
+            adj_n[i] = stage4.tile([P, NODES], BF16, name="adj_n")
+            nc.vector.tensor_scalar(
+                out=adj_n[i][:], in0=adj_raw[c][:, j, :], scalar1=dinv[c][:, j : j + 1], scalar2=None, op0=ALU.mult
             )
-            for j in range(CHUNK):
-                adj_n[c, j] = stage4.tile([P, NODES], BF16, name="adj_n")
-                nc.vector.tensor_scalar(
-                    out=adj_n[c, j][:],
-                    in0=adj_raw[c][:, j, :],
-                    scalar1=dinv[:, j : j + 1],
-                    scalar2=None,
-                    op0=ALU.mult,
+
+        def turn_adj(i):
+            words = adj_n[i][:].bitcast(F32)
+            for half in range(PASSES // 2):
+                bank = turned.tile([P, 2, 2, P], F32, tag="turned")
+                adj_turned[i, half] = bank
+                for g2 in range(2):
+                    for u in range(2):
+                        first = P * (2 * (2 * half + g2) + u)
+                        nc.tensor.transpose(out=bank[:, g2, u, :], in_=words[:, first : first + P], identity=ident[:])
+
+        def regroup_adj(i):
+            adj_grouped[i] = stage4.tile([P, PACK * K_PASS], BF16, name="adj_grouped", align_bytes=64)
+            grouped_words = adj_grouped[i][:].bitcast(F32).rearrange("p (g n u) -> p g n u", g=PASSES, u=2)
+            for half in range(PASSES // 2):
+                nc.scalar.copy(
+                    out=grouped_words[:, 2 * half : 2 * half + 2, :, :],
+                    in_=adj_turned[i, half][:].rearrange("p g u n -> p g n u"),
                 )
 
-        def turn_adj(c):
-            for j in range(CHUNK):
-                words = adj_n[c, j][:].bitcast(F32)
-                for half in range(PASSES // 2):
-                    bank = turned.tile([P, 2, 2, P], F32, tag="turned")
-                    adj_turned[c, j, half] = bank
-                    for g2 in range(2):
-                        for u in range(2):
-                            first = P * (2 * (2 * half + g2) + u)
-                            nc.tensor.transpose(
-                                out=bank[:, g2, u, :], in_=words[:, first : first + P], identity=ident[:]
-                            )
+        def quantise_adj(i):
+            nc.vector.quantize_mx(out=adj_codes[i][:].bitcast(FP8X4), scales=adj_scales[i][:], in_=adj_grouped[i][:])
 
-        def regroup_adj(c):
-            for j in range(CHUNK):
-                adj_grouped[c, j] = stage4.tile([P, PACK * K_PASS], BF16, name="adj_grouped", align_bytes=64)
-                grouped_words = adj_grouped[c, j][:].bitcast(F32).rearrange("p (g n u) -> p g n u", g=PASSES, u=2)
-                for half in range(PASSES // 2):
-                    nc.scalar.copy(
-                        out=grouped_words[:, 2 * half : 2 * half + 2, :, :],
-                        in_=adj_turned[c, j, half][:].rearrange("p g u n -> p g n u"),
-                    )
-
-        def quantise_adj(c):
-            for j in range(CHUNK):
-                i = CHUNK * c + j
-                nc.vector.quantize_mx(
-                    out=adj_codes[i][:].bitcast(FP8X4), scales=adj_scales[i][:], in_=adj_grouped[c, j][:]
+        def aggregate(i):
+            z_ps[i] = sums.tile([P, FEAT], F32, name="z_ps", tag="sums")
+            for g in range(PASSES):
+                row_cols = slice(P * g, P * (g + 1))
+                nc.tensor.matmul_mx(
+                    out=z_ps[i][:],
+                    lhsT=adj_codes[i][:, row_cols].bitcast(FP8X4),
+                    lhsT_scale=adj_scales[i][:, row_cols],
+                    rhs=h_codes[g][:].bitcast(FP8X4),
+                    rhs_scale=h_scales[g][:],
+                    start=(g == 0),
+                    stop=(g == PASSES - 1),
                 )
 
-        def aggregate(c):
-            for j in range(CHUNK):
-                i = CHUNK * c + j
-                z_ps[i] = sums.tile([P, FEAT], F32, name="z_ps", tag="sums")
-                for g in range(PASSES):
-                    row_cols = slice(P * g, P * (g + 1))
-                    nc.tensor.matmul_mx(
-                        out=z_ps[i][:],
-                        lhsT=adj_codes[i][:, row_cols].bitcast(FP8X4),
-                        lhsT_scale=adj_scales[i][:, row_cols],
-                        rhs=h_codes[g][:].bitcast(FP8X4),
-                        rhs_scale=h_scales[g][:],
-                        start=(g == 0),
-                        stop=(g == PASSES - 1),
-                    )
+        def finish(i):
+            result = stage4.tile([P, FEAT], F32, name="result")
+            nc.scalar.activation(out=result[:], in_=z_ps[i][:], func=ACT.Gelu, scale=mask_col[:, i : i + 1])
+            nc.sync.dma_start(out=out[0, P * i : P * (i + 1), :], in_=result[:])
 
-        def finish(c):
-            for j in range(CHUNK):
-                i = CHUNK * c + j
-                result = stage4.tile([P, FEAT], F32, name="result")
-                nc.scalar.activation(out=result[:], in_=z_ps[i][:], func=ACT.Gelu, scale=mask_col[:, i : i + 1])
-                nc.sync.dma_start(out=out[0, P * i : P * (i + 1), :], in_=result[:])
-
-        def in_range(c):
-            return 0 <= c < CHUNKS
+        def is_tile(i):
+            return 0 <= i < ROW_TILES
 
         turn_x(0)
         spread_bias_and_mask()
         quantise_x(0)
-        for r in range(-PASSES, CHUNKS + 1):
-            g = r + PASSES
-            if in_range(r + 1):
-                normalise(r + 1)
-            if g + 1 < PASSES:
+        for i in range(-H_LEAD, ROW_TILES + 1):
+            g, half = divmod(i + H_LEAD, 2)
+            next_x = half == 0 and g + 1 < PASSES
+            c, late = divmod(i + 3, CHUNK)
+            if next_x:
                 turn_x(g + 1)
+            if is_tile(i + 6):
+                sum_rows_scalar(i + 6)
+            if next_x:
                 quantise_x(g + 1)
+            if 0 <= c < CHUNKS:
+                invert_degree(c, 2 * late)
             if g < PASSES:
-                make_h(g)
-            if in_range(r - 1):
-                aggregate(r - 1)
-            if in_range(r + 1):
-                turn_adj(r + 1)
-            if in_range(r + 2):
-                sum_rows(r + 2)
-            if in_range(r - 1):
-                finish(r - 1)
-            if in_range(r + 1):
-                regroup_adj(r + 1)
-            if in_range(r):
-                quantise_adj(r)
+                make_h(g, 2 * half)
+            if is_tile(i + 5):
+                sum_rows_vector(i + 5)
+            if 0 <= c < CHUNKS:
+                invert_degree(c, 2 * late + 1)
+            if g < PASSES:
+                make_h(g, 2 * half + 1)
+            if is_tile(i):
+                quantise_adj(i)
+            if is_tile(i + 2):
+                normalise(i + 2)
+            if g < PASSES and half == 1:
+                quantise_h(g)
+            if is_tile(i - 1):
+                aggregate(i - 1)
+            if is_tile(i + 2):
+                turn_adj(i + 2)
+            if is_tile(i - 1):
+                finish(i - 1)
+            if is_tile(i + 2):
+                regroup_adj(i + 2)

@@ -19,11 +19,11 @@ NODES = 2048
 FEAT = 512
 PASSES = NODES // K_PASS
 ROW_TILES = NODES // P
-CHUNK = 2
-CHUNKS = ROW_TILES // CHUNK
 WORDS = NODES // 2
-SCALAR_ONLY_CHUNKS = 2
-VECTOR_SUM_COLS = 1536
+SCALAR_TILES = 4
+TENSOR_TILES = 4
+SCALAR_COLS = 512
+TINY = 2.0**-126
 H_LEAD = 9
 
 FLOPS = 2 * NODES * FEAT * FEAT + 2 * NODES * NODES * FEAT
@@ -41,6 +41,8 @@ def tile_graphconvlayer_pa_kernel(tc, x, mask, adj, W0_words, W0_scales, b0, out
 
         ident = keep.tile([P, P], F32)
         make_identity(nc, ident[:])
+        ident_bf16 = keep.tile([P, P], BF16)
+        make_identity(nc, ident_bf16[:])
         rows = keep.tile([P, FEAT + P], BF16)
         nc.vector.memset(rows[:], 0.0)
         nc.scalar.dma_start(out=rows[0:1, 0:FEAT], in_=b0.rearrange("(o f) -> o f", o=1))
@@ -55,14 +57,16 @@ def tile_graphconvlayer_pa_kernel(tc, x, mask, adj, W0_words, W0_scales, b0, out
         nc.scalar.activation(out=warm[:], in_=cold[:], func=ACT.Gelu)
 
         x_raw = [keep.tile([P, 2, 2 * FEAT], BF16, name="x_raw%d" % g) for g in range(PASSES)]
-        adj_raw = [keep.tile([P, CHUNK, NODES], BF16, name="adj_raw%d" % c) for c in range(CHUNKS)]
+        adj_raw = [keep.tile([P, NODES], BF16, name="adj_raw%d" % i) for i in range(ROW_TILES)]
         w_codes = keep.tile([P, FEAT], U32, align_bytes=64)
 
         def load_x(g):
-            nc.sync.dma_start(
-                out=x_raw[g][:],
-                in_=x[0, K_PASS * g : K_PASS * (g + 1), :].rearrange("(u j e) k -> j u (e k)", u=2, e=2),
-            )
+            nodes = x[0, K_PASS * g : K_PASS * (g + 1), :].rearrange("(u j e) k -> j u (e k)", u=2, e=2)
+            if g == 0:
+                for u in range(2):
+                    nc.sync.dma_start(out=x_raw[g][:, u, :], in_=nodes[:, u, :])
+            else:
+                nc.sync.dma_start(out=x_raw[g][:], in_=nodes)
 
         load_x(0)
         nc.sync.dma_start(
@@ -74,13 +78,13 @@ def tile_graphconvlayer_pa_kernel(tc, x, mask, adj, W0_words, W0_scales, b0, out
                 out=w_scales[32 * quadrant : 32 * quadrant + 4, :].bitcast(I32),
                 in_=W0_scales[0, 4 * quadrant : 4 * quadrant + 4, :].bitcast(I32),
             )
+        def load_adj(i):
+            nc.sync.dma_start(out=adj_raw[i][:], in_=adj[0, P * i : P * (i + 1), :])
+
         for g in range(1, PASSES):
             load_x(g)
-        for c in range(CHUNKS):
-            nc.sync.dma_start(
-                out=adj_raw[c][:],
-                in_=adj[0, CHUNK * P * c : CHUNK * P * (c + 1), :].rearrange("(j p) m -> p j m", p=P),
-            )
+        for i in range(ROW_TILES):
+            load_adj(i)
 
         bias = keep.tile([P, FEAT], F32)
         mask_col = keep.tile([P, ROW_TILES], F32)
@@ -118,7 +122,14 @@ def tile_graphconvlayer_pa_kernel(tc, x, mask, adj, W0_words, W0_scales, b0, out
                 )
 
         def quantise_x(g):
-            nc.vector.quantize_mx(out=x_codes[g][:].bitcast(FP8X4), scales=x_scales[g][:], in_=x_grouped[g][:])
+            parts = 2 if g == 0 else 1
+            for part in range(parts):
+                cols = slice(K_PASS * part // parts, K_PASS * (part + 1) // parts)
+                nc.vector.quantize_mx(
+                    out=x_codes[g][:, cols].bitcast(FP8X4),
+                    scales=x_scales[g][:, cols],
+                    in_=x_grouped[g][:, PACK * cols.start : PACK * cols.stop],
+                )
 
         h_grouped = {}
 
@@ -150,74 +161,80 @@ def tile_graphconvlayer_pa_kernel(tc, x, mask, adj, W0_words, W0_scales, b0, out
 
         adj_codes = [keep.tile([P, K_PASS], U32, name="adj_codes%d" % i, align_bytes=64) for i in range(ROW_TILES)]
         adj_scales = [keep.tile([P, K_PASS], U8, name="adj_scales%d" % i, align_bytes=64) for i in range(ROW_TILES)]
-        vector_sum = {}
         scalar_sum = {}
-        deg = {}
-        divisor = {}
-        inverse = {}
+        vector_sum = {}
         dinv = {}
+        folded = {}
         adj_n = {}
         adj_turned = {}
         adj_grouped = {}
         z_ps = {}
 
-        def vector_cols(c):
-            return 0 if c < SCALAR_ONLY_CHUNKS else VECTOR_SUM_COLS
+        def on_scalar(i):
+            return i < SCALAR_TILES
+
+        def on_tensor(i):
+            return SCALAR_TILES <= i < SCALAR_TILES + TENSOR_TILES
+
+        def column(tiles, i, name):
+            c, j = divmod(i, 2)
+            if c not in tiles:
+                tiles[c] = stage4.tile([P, 2], F32, name=name)
+            return tiles[c][:, j : j + 1]
 
         def sum_rows_scalar(i):
-            c, j = divmod(i, CHUNK)
-            if j == 0:
-                scalar_sum[c] = stage4.tile([P, CHUNK], F32, name="scalar_sum")
-            unread = stage2.tile([P, NODES - vector_cols(c)], BF16, name="unread_scalar")
+            cols = NODES if on_scalar(i) else SCALAR_COLS
+            unread = stage2.tile([P, NODES], BF16, name="unread_scalar")
             nc.scalar.activation(
-                out=unread[:],
-                in_=adj_raw[c][:, j, vector_cols(c) :],
+                out=unread[:, 0:cols],
+                in_=adj_raw[i][:, NODES - cols :],
                 func=ACT.Copy,
-                accum_out=scalar_sum[c][:, j : j + 1],
+                accum_out=column(scalar_sum, i, "scalar_sum"),
             )
+
+        def fold_rows(i):
+            folded[i] = sums.tile([P, P], F32, name="folded", tag="sums")
+            for block in range(NODES // P):
+                nc.tensor.matmul(
+                    out=folded[i][:],
+                    lhsT=ident_bf16[:],
+                    rhs=adj_raw[i][:, P * block : P * (block + 1)],
+                    start=(block == 0),
+                    stop=(block == NODES // P - 1),
+                )
 
         def sum_rows_vector(i):
-            c, j = divmod(i, CHUNK)
-            if vector_cols(c) == 0:
-                return
-            if j == 0:
-                vector_sum[c] = stage4.tile([P, CHUNK], F32, name="vector_sum")
-            unread = stage2.tile([P, vector_cols(c)], BF16, name="unread_vector")
+            source = folded[i][:] if on_tensor(i) else adj_raw[i][:, 0 : NODES - SCALAR_COLS]
+            unread = stage2.tile([P, NODES - SCALAR_COLS], BF16, name="unread_vector")
             nc.vector.tensor_scalar(
-                out=unread[:],
-                in0=adj_raw[c][:, j, 0 : vector_cols(c)],
+                out=unread[:, 0 : source.shape[1]],
+                in0=source,
                 scalar1=1.0,
-                scalar2=None,
+                scalar2=TINY,
                 op0=ALU.mult,
                 op1=ALU.add,
-                accum_out=vector_sum[c][:, j : j + 1],
+                accum_out=column(vector_sum, i, "vector_sum"),
             )
 
-        def invert_degree(c, step):
-            if step == 0:
-                deg[c] = scalar_sum[c]
-                if vector_cols(c) > 0:
-                    deg[c] = stage4.tile([P, CHUNK], F32, name="deg")
-                    nc.vector.tensor_tensor(out=deg[c][:], in0=vector_sum[c][:], in1=scalar_sum[c][:], op=ALU.add)
-            if step == 1:
-                divisor[c] = stage4.tile([P, CHUNK], F32, name="divisor")
-                nc.vector.scalar_tensor_tensor(
-                    out=divisor[c][:], in0=deg[c][:], scalar=0.0, in1=deg[c][:], op0=ALU.is_equal, op1=ALU.add
-                )
-            if step == 2:
-                inverse[c] = stage4.tile([P, CHUNK], F32, name="inverse")
-                nc.vector.reciprocal(out=inverse[c][:], in_=divisor[c][:])
-            if step == 3:
-                dinv[c] = stage4.tile([P, CHUNK], F32, name="dinv")
-                nc.vector.scalar_tensor_tensor(
-                    out=dinv[c][:], in0=deg[c][:], scalar=0.0, in1=inverse[c][:], op0=ALU.not_equal, op1=ALU.mult
-                )
+        def invert_degree(c):
+            if on_tensor(2 * c):
+                deg = vector_sum[c]
+            else:
+                deg = stage4.tile([P, 2], F32, name="deg")
+                if on_scalar(2 * c):
+                    nc.vector.tensor_scalar(
+                        out=deg[:], in0=scalar_sum[c][:], scalar1=TINY, scalar2=None, op0=ALU.add
+                    )
+                else:
+                    nc.vector.tensor_tensor(out=deg[:], in0=vector_sum[c][:], in1=scalar_sum[c][:], op=ALU.add)
+            dinv[c] = stage4.tile([P, 2], F32, name="dinv")
+            nc.vector.reciprocal(out=dinv[c][:], in_=deg[:])
 
         def normalise(i):
-            c, j = divmod(i, CHUNK)
+            c, j = divmod(i, 2)
             adj_n[i] = stage4.tile([P, NODES], BF16, name="adj_n")
             nc.vector.tensor_scalar(
-                out=adj_n[i][:], in0=adj_raw[c][:, j, :], scalar1=dinv[c][:, j : j + 1], scalar2=None, op0=ALU.mult
+                out=adj_n[i][:], in0=adj_raw[i][:], scalar1=dinv[c][:, j : j + 1], scalar2=None, op0=ALU.mult
             )
 
         def turn_adj(i):
@@ -267,37 +284,36 @@ def tile_graphconvlayer_pa_kernel(tc, x, mask, adj, W0_words, W0_scales, b0, out
         turn_x(0)
         spread_bias_and_mask()
         quantise_x(0)
-        for i in range(-H_LEAD, ROW_TILES + 1):
-            g, half = divmod(i + H_LEAD, 2)
-            next_x = half == 0 and g + 1 < PASSES
-            c, late = divmod(i + 3, CHUNK)
-            if next_x:
+        make_h(0, 0)
+        make_h(0, 1)
+        for r in range(-H_LEAD, ROW_TILES + 3):
+            g, half = divmod(r + H_LEAD, 2)
+            if half == 0 and g + 1 < PASSES:
                 turn_x(g + 1)
-            if is_tile(i + 6):
-                sum_rows_scalar(i + 6)
-            if next_x:
+            if is_tile(r):
+                quantise_adj(r)
+            if is_tile(r + 4) and r % 2:
+                invert_degree((r + 4) // 2)
+            if is_tile(r - 1):
+                aggregate(r - 1)
+            if is_tile(r - 3):
+                finish(r - 3)
+            if is_tile(r + 6) and not on_tensor(r + 6):
+                sum_rows_scalar(r + 6)
+            if is_tile(r + 5) and not on_scalar(r + 5):
+                sum_rows_vector(r + 5)
+            if half == 1 and g + 1 < PASSES:
                 quantise_x(g + 1)
-            if 0 <= c < CHUNKS:
-                invert_degree(c, 2 * late)
-            if g < PASSES:
+            if (g, half) != (0, 0) and g < PASSES:
                 make_h(g, 2 * half)
-            if is_tile(i + 5):
-                sum_rows_vector(i + 5)
-            if 0 <= c < CHUNKS:
-                invert_degree(c, 2 * late + 1)
-            if g < PASSES:
                 make_h(g, 2 * half + 1)
-            if is_tile(i):
-                quantise_adj(i)
-            if is_tile(i + 2):
-                normalise(i + 2)
-            if g < PASSES and half == 1:
-                quantise_h(g)
-            if is_tile(i - 1):
-                aggregate(i - 1)
-            if is_tile(i + 2):
-                turn_adj(i + 2)
-            if is_tile(i - 1):
-                finish(i - 1)
-            if is_tile(i + 2):
-                regroup_adj(i + 2)
+            if is_tile(r + 3):
+                normalise(r + 3)
+            if half == 1 and 0 <= g - 1 < PASSES:
+                quantise_h(g - 1)
+            if is_tile(r + 2):
+                turn_adj(r + 2)
+            if is_tile(r + 8) and on_tensor(r + 8):
+                fold_rows(r + 8)
+            if is_tile(r + 1):
+                regroup_adj(r + 1)

@@ -189,6 +189,7 @@ def tile_graphconvlayer_pa_kernel(tc, x, mask, adj, W0_words, W0_scales, b0, out
                 out=unread[:, 0:cols],
                 in_=adj_raw[i][:, NODES - cols :],
                 func=ACT.Copy,
+                bias=TINY,
                 accum_out=column(scalar_sum, i, "scalar_sum"),
             )
 
@@ -210,23 +211,14 @@ def tile_graphconvlayer_pa_kernel(tc, x, mask, adj, W0_words, W0_scales, b0, out
                 out=unread[:, 0 : source.shape[1]],
                 in0=source,
                 scalar1=1.0,
-                scalar2=TINY,
+                scalar2=TINY if on_tensor(i) else column(scalar_sum, i, "scalar_sum"),
                 op0=ALU.mult,
                 op1=ALU.add,
                 accum_out=column(vector_sum, i, "vector_sum"),
             )
 
         def invert_degree(c):
-            if on_tensor(2 * c):
-                deg = vector_sum[c]
-            else:
-                deg = stage4.tile([P, 2], F32, name="deg")
-                if on_scalar(2 * c):
-                    nc.vector.tensor_scalar(
-                        out=deg[:], in0=scalar_sum[c][:], scalar1=TINY, scalar2=None, op0=ALU.add
-                    )
-                else:
-                    nc.vector.tensor_tensor(out=deg[:], in0=vector_sum[c][:], in1=scalar_sum[c][:], op=ALU.add)
+            deg = scalar_sum[c] if on_scalar(2 * c) else vector_sum[c]
             dinv[c] = stage4.tile([P, 2], F32, name="dinv")
             nc.vector.reciprocal(out=dinv[c][:], in_=deg[:])
 
@@ -302,10 +294,11 @@ def tile_graphconvlayer_pa_kernel(tc, x, mask, adj, W0_words, W0_scales, b0, out
                 sum_rows_scalar(r + 6)
             if is_tile(r + 5) and not on_scalar(r + 5):
                 sum_rows_vector(r + 5)
+            if (g, half) != (0, 0) and g < PASSES:
+                make_h(g, 2 * half)
             if half == 1 and g + 1 < PASSES:
                 quantise_x(g + 1)
             if (g, half) != (0, 0) and g < PASSES:
-                make_h(g, 2 * half)
                 make_h(g, 2 * half + 1)
             if is_tile(r + 3):
                 normalise(r + 3)

@@ -22,7 +22,7 @@ ROW_TILES = NODES // P
 WORDS = NODES // 2
 SCALAR_TILES = 4
 TENSOR_TILES = 4
-SCALAR_COLS = 512
+SCALAR_COLS = 256
 TINY = 2.0**-126
 H_LEAD = 9
 

@@ -22,7 +22,7 @@ ROW_TILES = NODES // P
 WORDS = NODES // 2
 SCALAR_TILES = 4
 TENSOR_TILES = 4
-SCALAR_COLS = 256
+SCALAR_COLS = 384
 TINY = 2.0**-126
 H_LEAD = 9
 
@@ -34,6 +34,7 @@ def tile_graphconvlayer_pa_kernel(tc, x, mask, adj, W0_words, W0_scales, b0, out
     with ExitStack() as stack:
         keep = stack.enter_context(tc.tile_pool(name="keep", bufs=1))
         stage2 = stack.enter_context(tc.tile_pool(name="stage2", bufs=2))
+        stage6 = stack.enter_context(tc.tile_pool(name="stage6", bufs=6))
         stage4 = stack.enter_context(tc.tile_pool(name="stage4", bufs=4))
         turned = stack.enter_context(tc.psum_pool(name="turned", bufs=4))
         sums = stack.enter_context(tc.psum_pool(name="sums", bufs=4))
@@ -96,8 +97,8 @@ def tile_graphconvlayer_pa_kernel(tc, x, mask, adj, W0_words, W0_scales, b0, out
             nc.tensor.transpose(out=mask_ps[:], in_=mask_rows[:], identity=ident[:])
             bias_ps = sums.tile([P, FEAT], F32, tag="sums")
             nc.tensor.matmul(out=bias_ps[:], lhsT=ones[:], rhs=rows[:, 0:FEAT], start=True, stop=True)
-            nc.vector.tensor_copy(out=mask_col[:], in_=mask_ps[:, 0:ROW_TILES])
-            nc.vector.tensor_copy(out=bias[:], in_=bias_ps[:])
+            nc.scalar.copy(out=bias[:], in_=bias_ps[:])
+            nc.scalar.copy(out=mask_col[:], in_=mask_ps[:, 0:ROW_TILES])
 
         x_codes = [keep.tile([P, K_PASS], U32, name="x_codes%d" % g, align_bytes=64) for g in range(PASSES)]
         x_scales = [keep.tile([P, K_PASS], U8, name="x_scales%d" % g, align_bytes=64) for g in range(PASSES)]
@@ -251,61 +252,84 @@ def tile_graphconvlayer_pa_kernel(tc, x, mask, adj, W0_words, W0_scales, b0, out
         def quantise_adj(i):
             nc.vector.quantize_mx(out=adj_codes[i][:].bitcast(FP8X4), scales=adj_scales[i][:], in_=adj_grouped[i][:])
 
+        def parts_of(i):
+            return 2 if i == ROW_TILES - 1 else 1
+
+        def part_cols(i, part):
+            return slice(FEAT * part // parts_of(i), FEAT * (part + 1) // parts_of(i))
+
         def aggregate(i):
-            z_ps[i] = sums.tile([P, FEAT], F32, name="z_ps", tag="sums")
-            for g in range(PASSES):
-                row_cols = slice(P * g, P * (g + 1))
-                nc.tensor.matmul_mx(
-                    out=z_ps[i][:],
-                    lhsT=adj_codes[i][:, row_cols].bitcast(FP8X4),
-                    lhsT_scale=adj_scales[i][:, row_cols],
-                    rhs=h_codes[g][:].bitcast(FP8X4),
-                    rhs_scale=h_scales[g][:],
-                    start=(g == 0),
-                    stop=(g == PASSES - 1),
-                )
+            for part in range(parts_of(i)):
+                cols = part_cols(i, part)
+                z_ps[i, part] = sums.tile([P, cols.stop - cols.start], F32, name="z_ps", tag="sums")
+                for g in range(PASSES):
+                    row_cols = slice(P * g, P * (g + 1))
+                    nc.tensor.matmul_mx(
+                        out=z_ps[i, part][:],
+                        lhsT=adj_codes[i][:, row_cols].bitcast(FP8X4),
+                        lhsT_scale=adj_scales[i][:, row_cols],
+                        rhs=h_codes[g][:, cols].bitcast(FP8X4),
+                        rhs_scale=h_scales[g][:, cols],
+                        start=(g == 0),
+                        stop=(g == PASSES - 1),
+                    )
 
         def finish(i):
-            result = stage4.tile([P, FEAT], F32, name="result")
-            nc.scalar.activation(out=result[:], in_=z_ps[i][:], func=ACT.Gelu, scale=mask_col[:, i : i + 1])
-            nc.sync.dma_start(out=out[0, P * i : P * (i + 1), :], in_=result[:])
+            for part in range(parts_of(i)):
+                cols = part_cols(i, part)
+                result = stage6.tile([P, cols.stop - cols.start], F32, name="result")
+                nc.scalar.activation(
+                    out=result[:], in_=z_ps[i, part][:], func=ACT.Gelu, scale=mask_col[:, i : i + 1]
+                )
+                nc.sync.dma_start(out=out[0, P * i : P * (i + 1), cols], in_=result[:])
 
         def is_tile(i):
             return 0 <= i < ROW_TILES
 
+        def turn_round(i):
+            return ROW_TILES - 4 if i >= ROW_TILES - 2 else i - 2
+
+        def pass_round(i):
+            return ROW_TILES + 1 if i >= ROW_TILES - 2 else i + 1
+
         turn_x(0)
         spread_bias_and_mask()
         quantise_x(0)
-        make_h(0, 0)
-        make_h(0, 1)
+        for block in range(PACK):
+            make_h(0, block)
+        turn_x(1)
+        quantise_h(0)
+        quantise_x(1)
         for r in range(-H_LEAD, ROW_TILES + 3):
             g, half = divmod(r + H_LEAD, 2)
-            if half == 0 and g + 1 < PASSES:
+            if half == 0 and 0 < g < PASSES - 1:
                 turn_x(g + 1)
             if is_tile(r):
                 quantise_adj(r)
             if is_tile(r + 4) and r % 2:
                 invert_degree((r + 4) // 2)
-            if is_tile(r - 1):
-                aggregate(r - 1)
+            for i in range(ROW_TILES):
+                if pass_round(i) == r:
+                    aggregate(i)
             if is_tile(r - 3):
                 finish(r - 3)
             if is_tile(r + 6) and not on_tensor(r + 6):
                 sum_rows_scalar(r + 6)
             if is_tile(r + 5) and not on_scalar(r + 5):
                 sum_rows_vector(r + 5)
-            if (g, half) != (0, 0) and g < PASSES:
+            if 0 < g < PASSES:
                 make_h(g, 2 * half)
-            if half == 1 and g + 1 < PASSES:
+            if half == 1 and 0 < g < PASSES - 1:
                 quantise_x(g + 1)
-            if (g, half) != (0, 0) and g < PASSES:
+            if 0 < g < PASSES:
                 make_h(g, 2 * half + 1)
             if is_tile(r + 3):
                 normalise(r + 3)
-            if half == 1 and 0 <= g - 1 < PASSES:
+            if half == 1 and 0 < g - 1 < PASSES:
                 quantise_h(g - 1)
-            if is_tile(r + 2):
-                turn_adj(r + 2)
+            for i in range(ROW_TILES):
+                if turn_round(i) == r:
+                    turn_adj(i)
             if is_tile(r + 8) and on_tensor(r + 8):
                 fold_rows(r + 8)
             if is_tile(r + 1):

@@ -22,7 +22,7 @@ ROW_TILES = NODES // P
 WORDS = NODES // 2
 SCALAR_TILES = 4
 TENSOR_TILES = 4
-SCALAR_COLS = 384
+SCALAR_COLS = 416
 TINY = 2.0**-126
 H_LEAD = 9
 
@@ -109,21 +109,23 @@ def tile_graphconvlayer_pa_kernel(tc, x, mask, adj, W0_words, W0_scales, b0, out
         def turn_x(g):
             x_grouped[g] = stage2.tile([P, PACK * K_PASS], BF16, name="x_grouped", align_bytes=64)
             grouped_words = x_grouped[g][:].bitcast(F32).rearrange("p (t j v) -> p t j v", t=PACK, v=2)
-            for u in range(2):
-                x_turned = turned.tile([P, 2, 2, P], F32, tag="turned")
-                for e in range(2):
+            sets = 1 if g == 0 else 2
+            for t in range(0, PACK, sets):
+                x_turned = turned.tile([P, sets, 2, P], F32, tag="turned")
+                for s in range(sets):
+                    u, e = divmod(t + s, 2)
                     words = x_raw[g][:, u, FEAT * e : FEAT * (e + 1)].bitcast(F32)
                     for v in range(2):
                         nc.tensor.transpose(
-                            out=x_turned[:, e, v, :], in_=words[:, v : FEAT // 2 : 2], identity=ident[:]
+                            out=x_turned[:, s, v, :], in_=words[:, v : FEAT // 2 : 2], identity=ident[:]
                         )
                 nc.scalar.copy(
-                    out=grouped_words[:, 2 * u : 2 * u + 2, :, :],
-                    in_=x_turned[:].rearrange("p e v j -> p e j v"),
+                    out=grouped_words[:, t : t + sets, :, :],
+                    in_=x_turned[:].rearrange("p s v j -> p s j v"),
                 )
 
         def quantise_x(g):
-            parts = 2 if g == 0 else 1
+            parts = PACK if g == 0 else 1
             for part in range(parts):
                 cols = slice(K_PASS * part // parts, K_PASS * (part + 1) // parts)
                 nc.vector.quantize_mx(
@@ -177,21 +179,16 @@ def tile_graphconvlayer_pa_kernel(tc, x, mask, adj, W0_words, W0_scales, b0, out
         def on_tensor(i):
             return SCALAR_TILES <= i < SCALAR_TILES + TENSOR_TILES
 
-        def column(tiles, i, name):
-            c, j = divmod(i, 2)
-            if c not in tiles:
-                tiles[c] = stage4.tile([P, 2], F32, name=name)
-            return tiles[c][:, j : j + 1]
-
         def sum_rows_scalar(i):
             cols = NODES if on_scalar(i) else SCALAR_COLS
             unread = stage2.tile([P, NODES], BF16, name="unread_scalar")
+            scalar_sum[i] = stage6.tile([P, 1], F32, name="scalar_sum")
             nc.scalar.activation(
                 out=unread[:, 0:cols],
                 in_=adj_raw[i][:, NODES - cols :],
                 func=ACT.Copy,
                 bias=TINY,
-                accum_out=column(scalar_sum, i, "scalar_sum"),
+                accum_out=scalar_sum[i][:],
             )
 
         def fold_rows(i):
@@ -208,26 +205,26 @@ def tile_graphconvlayer_pa_kernel(tc, x, mask, adj, W0_words, W0_scales, b0, out
         def sum_rows_vector(i):
             source = folded[i][:] if on_tensor(i) else adj_raw[i][:, 0 : NODES - SCALAR_COLS]
             unread = stage2.tile([P, NODES - SCALAR_COLS], BF16, name="unread_vector")
+            vector_sum[i] = stage6.tile([P, 1], F32, name="vector_sum")
             nc.vector.tensor_scalar(
                 out=unread[:, 0 : source.shape[1]],
                 in0=source,
                 scalar1=1.0,
-                scalar2=TINY if on_tensor(i) else column(scalar_sum, i, "scalar_sum"),
+                scalar2=TINY if on_tensor(i) else scalar_sum[i][:],
                 op0=ALU.mult,
                 op1=ALU.add,
-                accum_out=column(vector_sum, i, "vector_sum"),
+                accum_out=vector_sum[i][:],
             )
 
-        def invert_degree(c):
-            deg = scalar_sum[c] if on_scalar(2 * c) else vector_sum[c]
-            dinv[c] = stage4.tile([P, 2], F32, name="dinv")
-            nc.vector.reciprocal(out=dinv[c][:], in_=deg[:])
+        def invert_degree(i):
+            deg = scalar_sum[i] if on_scalar(i) else vector_sum[i]
+            dinv[i] = stage6.tile([P, 1], F32, name="dinv")
+            nc.vector.reciprocal(out=dinv[i][:], in_=deg[:])
 
         def normalise(i):
-            c, j = divmod(i, 2)
             adj_n[i] = stage4.tile([P, NODES], BF16, name="adj_n")
             nc.vector.tensor_scalar(
-                out=adj_n[i][:], in0=adj_raw[i][:], scalar1=dinv[c][:, j : j + 1], scalar2=None, op0=ALU.mult
+                out=adj_n[i][:], in0=adj_raw[i][:], scalar1=dinv[i][:], scalar2=None, op0=ALU.mult
             )
 
         def turn_adj(i):
@@ -286,12 +283,6 @@ def tile_graphconvlayer_pa_kernel(tc, x, mask, adj, W0_words, W0_scales, b0, out
         def is_tile(i):
             return 0 <= i < ROW_TILES
 
-        def turn_round(i):
-            return ROW_TILES - 4 if i >= ROW_TILES - 2 else i - 2
-
-        def pass_round(i):
-            return ROW_TILES + 1 if i >= ROW_TILES - 2 else i + 1
-
         turn_x(0)
         spread_bias_and_mask()
         quantise_x(0)
@@ -306,17 +297,19 @@ def tile_graphconvlayer_pa_kernel(tc, x, mask, adj, W0_words, W0_scales, b0, out
                 turn_x(g + 1)
             if is_tile(r):
                 quantise_adj(r)
-            if is_tile(r + 4) and r % 2:
-                invert_degree((r + 4) // 2)
-            for i in range(ROW_TILES):
-                if pass_round(i) == r:
-                    aggregate(i)
+            turn_first = r > 0 and r % 2 == 1
+            if turn_first and is_tile(r + 2):
+                turn_adj(r + 2)
+            if is_tile(r - 1):
+                aggregate(r - 1)
             if is_tile(r - 3):
                 finish(r - 3)
-            if is_tile(r + 6) and not on_tensor(r + 6):
+            if is_tile(r + 6) and on_scalar(r + 6):
                 sum_rows_scalar(r + 6)
-            if is_tile(r + 5) and not on_scalar(r + 5):
-                sum_rows_vector(r + 5)
+            if is_tile(r + 5) and not on_scalar(r + 5) and not on_tensor(r + 5):
+                sum_rows_scalar(r + 5)
+            if is_tile(r + 4) and not on_scalar(r + 4):
+                sum_rows_vector(r + 4)
             if 0 < g < PASSES:
                 make_h(g, 2 * half)
             if half == 1 and 0 < g < PASSES - 1:
@@ -325,11 +318,12 @@ def tile_graphconvlayer_pa_kernel(tc, x, mask, adj, W0_words, W0_scales, b0, out
                 make_h(g, 2 * half + 1)
             if is_tile(r + 3):
                 normalise(r + 3)
+            if is_tile(r + 4):
+                invert_degree(r + 4)
             if half == 1 and 0 < g - 1 < PASSES:
                 quantise_h(g - 1)
-            for i in range(ROW_TILES):
-                if turn_round(i) == r:
-                    turn_adj(i)
+            if not turn_first and is_tile(r + 2):
+                turn_adj(r + 2)
             if is_tile(r + 8) and on_tensor(r + 8):
                 fold_rows(r + 8)
             if is_tile(r + 1):

@@ -20,9 +20,9 @@ FEAT = 512
 PASSES = NODES // K_PASS
 ROW_TILES = NODES // P
 WORDS = NODES // 2
-SCALAR_TILES = 4
+SCALAR_TILES = 3
 TENSOR_TILES = 4
-SCALAR_COLS = 416
+SCALAR_COLS = 320
 TINY = 2.0**-126
 H_LEAD = 9
 
@@ -125,7 +125,7 @@ def tile_graphconvlayer_pa_kernel(tc, x, mask, adj, W0_words, W0_scales, b0, out
                 )
 
         def quantise_x(g):
-            parts = PACK if g == 0 else 1
+            parts = {0: PACK, 1: 2}.get(g, 1)
             for part in range(parts):
                 cols = slice(K_PASS * part // parts, K_PASS * (part + 1) // parts)
                 nc.vector.quantize_mx(
@@ -289,8 +289,8 @@ def tile_graphconvlayer_pa_kernel(tc, x, mask, adj, W0_words, W0_scales, b0, out
         for block in range(PACK):
             make_h(0, block)
         turn_x(1)
-        quantise_h(0)
         quantise_x(1)
+        quantise_h(0)
         for r in range(-H_LEAD, ROW_TILES + 3):
             g, half = divmod(r + H_LEAD, 2)
             if half == 0 and 0 < g < PASSES - 1:
@@ -324,7 +324,7 @@ def tile_graphconvlayer_pa_kernel(tc, x, mask, adj, W0_words, W0_scales, b0, out
                 quantise_h(g - 1)
             if not turn_first and is_tile(r + 2):
                 turn_adj(r + 2)
-            if is_tile(r + 8) and on_tensor(r + 8):
-                fold_rows(r + 8)
+            if is_tile(r + 7) and on_tensor(r + 7):
+                fold_rows(r + 7)
             if is_tile(r + 1):
                 regroup_adj(r + 1)

@@ -22,7 +22,7 @@ ROW_TILES = NODES // P
 WORDS = NODES // 2
 SCALAR_TILES = 3
 TENSOR_TILES = 4
-SCALAR_COLS = 320
+SCALAR_COLS = 416
 TINY = 2.0**-126
 H_LEAD = 9
 
@@ -181,11 +181,12 @@ def tile_graphconvlayer_pa_kernel(tc, x, mask, adj, W0_words, W0_scales, b0, out
 
         def sum_rows_scalar(i):
             cols = NODES if on_scalar(i) else SCALAR_COLS
+            source = folded[i][:] if on_tensor(i) else adj_raw[i][:, NODES - cols :]
             unread = stage2.tile([P, NODES], BF16, name="unread_scalar")
             scalar_sum[i] = stage6.tile([P, 1], F32, name="scalar_sum")
             nc.scalar.activation(
-                out=unread[:, 0:cols],
-                in_=adj_raw[i][:, NODES - cols :],
+                out=unread[:, 0 : source.shape[1]],
+                in_=source,
                 func=ACT.Copy,
                 bias=TINY,
                 accum_out=scalar_sum[i][:],
@@ -203,21 +204,20 @@ def tile_graphconvlayer_pa_kernel(tc, x, mask, adj, W0_words, W0_scales, b0, out
                 )
 
         def sum_rows_vector(i):
-            source = folded[i][:] if on_tensor(i) else adj_raw[i][:, 0 : NODES - SCALAR_COLS]
             unread = stage2.tile([P, NODES - SCALAR_COLS], BF16, name="unread_vector")
             vector_sum[i] = stage6.tile([P, 1], F32, name="vector_sum")
             nc.vector.tensor_scalar(
-                out=unread[:, 0 : source.shape[1]],
-                in0=source,
+                out=unread[:],
+                in0=adj_raw[i][:, 0 : NODES - SCALAR_COLS],
                 scalar1=1.0,
-                scalar2=TINY if on_tensor(i) else scalar_sum[i][:],
+                scalar2=scalar_sum[i][:],
                 op0=ALU.mult,
                 op1=ALU.add,
                 accum_out=vector_sum[i][:],
             )
 
         def invert_degree(i):
-            deg = scalar_sum[i] if on_scalar(i) else vector_sum[i]
+            deg = scalar_sum[i] if on_scalar(i) or on_tensor(i) else vector_sum[i]
             dinv[i] = stage6.tile([P, 1], F32, name="dinv")
             nc.vector.reciprocal(out=dinv[i][:], in_=deg[:])
 
@@ -308,7 +308,9 @@ def tile_graphconvlayer_pa_kernel(tc, x, mask, adj, W0_words, W0_scales, b0, out
                 sum_rows_scalar(r + 6)
             if is_tile(r + 5) and not on_scalar(r + 5) and not on_tensor(r + 5):
                 sum_rows_scalar(r + 5)
-            if is_tile(r + 4) and not on_scalar(r + 4):
+            if is_tile(r + 4) and on_tensor(r + 4):
+                sum_rows_scalar(r + 4)
+            if is_tile(r + 4) and not on_scalar(r + 4) and not on_tensor(r + 4):
                 sum_rows_vector(r + 4)
             if 0 < g < PASSES:
                 make_h(g, 2 * half)

@@ -24,6 +24,7 @@ SCALAR_TILES = 3
 TENSOR_TILES = 4
 SCALAR_COLS = 416
 TINY = 2.0**-126
+WARM_UP = 7
 H_LEAD = 9
 
 FLOPS = 2 * NODES * FEAT * FEAT + 2 * NODES * NODES * FEAT
@@ -40,18 +41,23 @@ def tile_graphconvlayer_pa_kernel(tc, x, mask, adj, W0_words, W0_scales, b0, out
         sums = stack.enter_context(tc.psum_pool(name="sums", bufs=4))
         stack.enter_context(tc.manual_schedule())
 
+        zeros = keep.tile([P, 2 * P], BF16)
+        nc.gpsimd.memset(zeros[:], 0.0)
+        for i in range(WARM_UP):
+            unread_ps = sums.tile([P, 2 * P], F32, name="unread_ps", tag="sums")
+            nc.tensor.matmul(out=unread_ps[:], lhsT=zeros[:, 0:P], rhs=zeros[:], start=True, stop=True)
         ident = keep.tile([P, P], F32)
         make_identity(nc, ident[:])
         ident_bf16 = keep.tile([P, P], BF16)
         make_identity(nc, ident_bf16[:])
+        w_scales = keep.tile([P, FEAT], U8, align_bytes=64)
+        nc.vector.memset(w_scales[:].bitcast(I32), 0)
         rows = keep.tile([P, FEAT + P], BF16)
         nc.vector.memset(rows[:], 0.0)
         nc.scalar.dma_start(out=rows[0:1, 0:FEAT], in_=b0.rearrange("(o f) -> o f", o=1))
         nc.scalar.dma_start(out=rows[0:ROW_TILES, FEAT:], in_=mask[0].rearrange("(i p) -> i p", p=P))
         ones = keep.tile([P, P], BF16)
         nc.vector.memset(ones[:], 1.0)
-        w_scales = keep.tile([P, FEAT], U8, align_bytes=64)
-        nc.vector.memset(w_scales[:].bitcast(I32), 0)
         cold = keep.tile([P, 1], F32)
         nc.vector.memset(cold[:], 0.0)
         warm = keep.tile([P, 1], F32)

from contextlib import ExitStack

import concourse.mybir as mybir
from concourse.masks import make_identity

F32 = mybir.dt.float32
BF16 = mybir.dt.bfloat16
I32 = mybir.dt.int32
U32 = mybir.dt.uint32
U8 = mybir.dt.uint8
FP8X4 = mybir.dt.float8_e4m3fn_x4
ALU = mybir.AluOpType
ACT = mybir.ActivationFunctionType

P = 128
PACK = 4
K_PASS = P * PACK
NODES = 2048
FEAT = 512
PASSES = NODES // K_PASS
ROW_TILES = NODES // P
WORDS = NODES // 2
SCALAR_TILES = 3
TENSOR_TILES = 4
SCALAR_COLS = 416
TINY = 2.0**-126
WARM_UP = 7
H_LEAD = 9

FLOPS = 2 * NODES * FEAT * FEAT + 2 * NODES * NODES * FEAT


def tile_graphconvlayer_pa_kernel(tc, x, mask, adj, W0_words, W0_scales, b0, out):
    nc = tc.nc
    with ExitStack() as stack:
        keep = stack.enter_context(tc.tile_pool(name="keep", bufs=1))
        stage2 = stack.enter_context(tc.tile_pool(name="stage2", bufs=2))
        stage6 = stack.enter_context(tc.tile_pool(name="stage6", bufs=6))
        stage4 = stack.enter_context(tc.tile_pool(name="stage4", bufs=4))
        turned = stack.enter_context(tc.psum_pool(name="turned", bufs=4))
        sums = stack.enter_context(tc.psum_pool(name="sums", bufs=4))
        stack.enter_context(tc.manual_schedule())

        zeros = keep.tile([P, 2 * P], BF16)
        nc.gpsimd.memset(zeros[:], 0.0)
        for i in range(WARM_UP):
            unread_ps = sums.tile([P, 2 * P], F32, name="unread_ps", tag="sums")
            nc.tensor.matmul(out=unread_ps[:], lhsT=zeros[:, 0:P], rhs=zeros[:], start=True, stop=True)
        ident = keep.tile([P, P], F32)
        make_identity(nc, ident[:])
        ident_bf16 = keep.tile([P, P], BF16)
        make_identity(nc, ident_bf16[:])
        w_scales = keep.tile([P, FEAT], U8, align_bytes=64)
        nc.vector.memset(w_scales[:].bitcast(I32), 0)
        rows = keep.tile([P, FEAT + P], BF16)
        nc.vector.memset(rows[:], 0.0)
        nc.scalar.dma_start(out=rows[0:1, 0:FEAT], in_=b0.rearrange("(o f) -> o f", o=1))
        nc.scalar.dma_start(out=rows[0:ROW_TILES, FEAT:], in_=mask[0].rearrange("(i p) -> i p", p=P))
        ones = keep.tile([P, P], BF16)
        nc.vector.memset(ones[:], 1.0)
        cold = keep.tile([P, 1], F32)
        nc.vector.memset(cold[:], 0.0)
        warm = keep.tile([P, 1], F32)
        nc.scalar.activation(out=warm[:], in_=cold[:], func=ACT.Gelu)

        x_raw = [keep.tile([P, 2, 2 * FEAT], BF16, name="x_raw%d" % g) for g in range(PASSES)]
        adj_raw = [keep.tile([P, NODES], BF16, name="adj_raw%d" % i) for i in range(ROW_TILES)]
        w_codes = keep.tile([P, FEAT], U32, align_bytes=64)

        def load_x(g):
            nodes = x[0, K_PASS * g : K_PASS * (g + 1), :].rearrange("(u j e) k -> j u (e k)", u=2, e=2)
            if g == 0:
                for u in range(2):
                    nc.sync.dma_start(out=x_raw[g][:, u, :], in_=nodes[:, u, :])
            else:
                nc.sync.dma_start(out=x_raw[g][:], in_=nodes)

        load_x(0)
        nc.sync.dma_start(
            out=w_codes[:].bitcast(I32),
            in_=W0_words[0].rearrange("p n t -> p (n t)").bitcast(I32),
        )
        for quadrant in range(4):
            nc.sync.dma_start(
                out=w_scales[32 * quadrant : 32 * quadrant + 4, :].bitcast(I32),
                in_=W0_scales[0, 4 * quadrant : 4 * quadrant + 4, :].bitcast(I32),
            )
        def load_adj(i):
            nc.sync.dma_start(out=adj_raw[i][:], in_=adj[0, P * i : P * (i + 1), :])

        for g in range(1, PASSES):
            load_x(g)
        for i in range(ROW_TILES):
            load_adj(i)

        bias = keep.tile([P, FEAT], F32)
        mask_col = keep.tile([P, ROW_TILES], F32)

        def spread_bias_and_mask():
            mask_rows = keep.tile([P, P], F32)
            nc.vector.tensor_copy(out=mask_rows[:], in_=rows[:, FEAT:])
            mask_ps = turned.tile([P, P], F32, tag="turned")
            nc.tensor.transpose(out=mask_ps[:], in_=mask_rows[:], identity=ident[:])
            bias_ps = sums.tile([P, FEAT], F32, tag="sums")
            nc.tensor.matmul(out=bias_ps[:], lhsT=ones[:], rhs=rows[:, 0:FEAT], start=True, stop=True)
            nc.scalar.copy(out=bias[:], in_=bias_ps[:])
            nc.scalar.copy(out=mask_col[:], in_=mask_ps[:, 0:ROW_TILES])

        x_codes = [keep.tile([P, K_PASS], U32, name="x_codes%d" % g, align_bytes=64) for g in range(PASSES)]
        x_scales = [keep.tile([P, K_PASS], U8, name="x_scales%d" % g, align_bytes=64) for g in range(PASSES)]
        h_codes = [keep.tile([P, FEAT], U32, name="h_codes%d" % g, align_bytes=64) for g in range(PASSES)]
        h_scales = [keep.tile([P, FEAT], U8, name="h_scales%d" % g, align_bytes=64) for g in range(PASSES)]
        x_grouped = {}

        def turn_x(g):
            x_grouped[g] = stage2.tile([P, PACK * K_PASS], BF16, name="x_grouped", align_bytes=64)
            grouped_words = x_grouped[g][:].bitcast(F32).rearrange("p (t j v) -> p t j v", t=PACK, v=2)
            sets = 1 if g == 0 else 2
            for t in range(0, PACK, sets):
                x_turned = turned.tile([P, sets, 2, P], F32, tag="turned")
                for s in range(sets):
                    u, e = divmod(t + s, 2)
                    words = x_raw[g][:, u, FEAT * e : FEAT * (e + 1)].bitcast(F32)
                    for v in range(2):
                        nc.tensor.transpose(
                            out=x_turned[:, s, v, :], in_=words[:, v : FEAT // 2 : 2], identity=ident[:]
                        )
                nc.scalar.copy(
                    out=grouped_words[:, t : t + sets, :, :],
                    in_=x_turned[:].rearrange("p s v j -> p s j v"),
                )

        def quantise_x(g):
            parts = {0: PACK, 1: 2}.get(g, 1)
            for part in range(parts):
                cols = slice(K_PASS * part // parts, K_PASS * (part + 1) // parts)
                nc.vector.quantize_mx(
                    out=x_codes[g][:, cols].bitcast(FP8X4),
                    scales=x_scales[g][:, cols],
                    in_=x_grouped[g][:, PACK * cols.start : PACK * cols.stop],
                )

        h_grouped = {}

        def make_h(g, block):
            if block == 0:
                h_grouped[g] = stage2.tile([P, PACK * FEAT], BF16, name="h_grouped", align_bytes=64)
            f_cols = slice(P * block, P * (block + 1))
            h_ps = sums.tile([P, PACK, P], F32, tag="sums")
            for t in range(PACK):
                node_cols = slice(P * t, P * (t + 1))
                nc.tensor.matmul_mx(
                    out=h_ps[:, t, :],
                    lhsT=x_codes[g][:, node_cols].bitcast(FP8X4),
                    lhsT_scale=x_scales[g][:, node_cols],
                    rhs=w_codes[:, f_cols].bitcast(FP8X4),
                    rhs_scale=w_scales[:, f_cols],
                    start=True,
                    stop=True,
                )
            nc.vector.tensor_tensor(
                out=h_grouped[g][:].rearrange("p (f t) -> p f t", t=PACK)[:, f_cols, :],
                in0=h_ps[:].rearrange("p t f -> p f t"),
                in1=bias[:, f_cols].unsqueeze(2).to_broadcast([P, P, PACK]),
                op=ALU.add,
            )

        def quantise_h(g):
            nc.vector.quantize_mx(out=h_codes[g][:].bitcast(FP8X4), scales=h_scales[g][:], in_=h_grouped[g][:])

        adj_codes = [keep.tile([P, K_PASS], U32, name="adj_codes%d" % i, align_bytes=64) for i in range(ROW_TILES)]
        adj_scales = [keep.tile([P, K_PASS], U8, name="adj_scales%d" % i, align_bytes=64) for i in range(ROW_TILES)]
        scalar_sum = {}
        vector_sum = {}
        dinv = {}
        folded = {}
        adj_n = {}
        adj_turned = {}
        adj_grouped = {}
        z_ps = {}

        def on_scalar(i):
            return i < SCALAR_TILES

        def on_tensor(i):
            return SCALAR_TILES <= i < SCALAR_TILES + TENSOR_TILES

        def sum_rows_scalar(i):
            cols = NODES if on_scalar(i) else SCALAR_COLS
            source = folded[i][:] if on_tensor(i) else adj_raw[i][:, NODES - cols :]
            unread = stage2.tile([P, NODES], BF16, name="unread_scalar")
            scalar_sum[i] = stage6.tile([P, 1], F32, name="scalar_sum")
            nc.scalar.activation(
                out=unread[:, 0 : source.shape[1]],
                in_=source,
                func=ACT.Copy,
                bias=TINY,
                accum_out=scalar_sum[i][:],
            )

        def fold_rows(i):
            folded[i] = sums.tile([P, P], F32, name="folded", tag="sums")
            for block in range(NODES // P):
                nc.tensor.matmul(
                    out=folded[i][:],
                    lhsT=ident_bf16[:],
                    rhs=adj_raw[i][:, P * block : P * (block + 1)],
                    start=(block == 0),
                    stop=(block == NODES // P - 1),
                )

        def sum_rows_vector(i):
            unread = stage2.tile([P, NODES - SCALAR_COLS], BF16, name="unread_vector")
            vector_sum[i] = stage6.tile([P, 1], F32, name="vector_sum")
            nc.vector.tensor_scalar(
                out=unread[:],
                in0=adj_raw[i][:, 0 : NODES - SCALAR_COLS],
                scalar1=1.0,
                scalar2=scalar_sum[i][:],
                op0=ALU.mult,
                op1=ALU.add,
                accum_out=vector_sum[i][:],
            )

        def invert_degree(i):
            deg = scalar_sum[i] if on_scalar(i) or on_tensor(i) else vector_sum[i]
            dinv[i] = stage6.tile([P, 1], F32, name="dinv")
            nc.vector.reciprocal(out=dinv[i][:], in_=deg[:])

        def normalise(i):
            adj_n[i] = stage4.tile([P, NODES], BF16, name="adj_n")
            nc.vector.tensor_scalar(
                out=adj_n[i][:], in0=adj_raw[i][:], scalar1=dinv[i][:], scalar2=None, op0=ALU.mult
            )

        def turn_adj(i):
            words = adj_n[i][:].bitcast(F32)
            for half in range(PASSES // 2):
                bank = turned.tile([P, 2, 2, P], F32, tag="turned")
                adj_turned[i, half] = bank
                for g2 in range(2):
                    for u in range(2):
                        first = P * (2 * (2 * half + g2) + u)
                        nc.tensor.transpose(out=bank[:, g2, u, :], in_=words[:, first : first + P], identity=ident[:])

        def regroup_adj(i):
            adj_grouped[i] = stage4.tile([P, PACK * K_PASS], BF16, name="adj_grouped", align_bytes=64)
            grouped_words = adj_grouped[i][:].bitcast(F32).rearrange("p (g n u) -> p g n u", g=PASSES, u=2)
            for half in range(PASSES // 2):
                nc.scalar.copy(
                    out=grouped_words[:, 2 * half : 2 * half + 2, :, :],
                    in_=adj_turned[i, half][:].rearrange("p g u n -> p g n u"),
                )

        def quantise_adj(i):
            nc.vector.quantize_mx(out=adj_codes[i][:].bitcast(FP8X4), scales=adj_scales[i][:], in_=adj_grouped[i][:])

        def parts_of(i):
            return 2 if i == ROW_TILES - 1 else 1

        def part_cols(i, part):
            return slice(FEAT * part // parts_of(i), FEAT * (part + 1) // parts_of(i))

        def aggregate(i):
            for part in range(parts_of(i)):
                cols = part_cols(i, part)
                z_ps[i, part] = sums.tile([P, cols.stop - cols.start], F32, name="z_ps", tag="sums")
                for g in range(PASSES):
                    row_cols = slice(P * g, P * (g + 1))
                    nc.tensor.matmul_mx(
                        out=z_ps[i, part][:],
                        lhsT=adj_codes[i][:, row_cols].bitcast(FP8X4),
                        lhsT_scale=adj_scales[i][:, row_cols],
                        rhs=h_codes[g][:, cols].bitcast(FP8X4),
                        rhs_scale=h_scales[g][:, cols],
                        start=(g == 0),
                        stop=(g == PASSES - 1),
                    )

        def finish(i):
            for part in range(parts_of(i)):
                cols = part_cols(i, part)
                result = stage6.tile([P, cols.stop - cols.start], F32, name="result")
                nc.scalar.activation(
                    out=result[:], in_=z_ps[i, part][:], func=ACT.Gelu, scale=mask_col[:, i : i + 1]
                )
                nc.sync.dma_start(out=out[0, P * i : P * (i + 1), cols], in_=result[:])

        def is_tile(i):
            return 0 <= i < ROW_TILES

        turn_x(0)
        spread_bias_and_mask()
        quantise_x(0)
        for block in range(PACK):
            make_h(0, block)
        turn_x(1)
        quantise_x(1)
        quantise_h(0)
        for r in range(-H_LEAD, ROW_TILES + 3):
            g, half = divmod(r + H_LEAD, 2)
            if half == 0 and 0 < g < PASSES - 1:
                turn_x(g + 1)
            if is_tile(r):
                quantise_adj(r)
            turn_first = r > 0 and r % 2 == 1
            if turn_first and is_tile(r + 2):
                turn_adj(r + 2)
            if is_tile(r - 1):
                aggregate(r - 1)
            if is_tile(r - 3):
                finish(r - 3)
            if is_tile(r + 6) and on_scalar(r + 6):
                sum_rows_scalar(r + 6)
            if is_tile(r + 5) and not on_scalar(r + 5) and not on_tensor(r + 5):
                sum_rows_scalar(r + 5)
            if is_tile(r + 4) and on_tensor(r + 4):
                sum_rows_scalar(r + 4)
            if is_tile(r + 4) and not on_scalar(r + 4) and not on_tensor(r + 4):
                sum_rows_vector(r + 4)
            if 0 < g < PASSES:
                make_h(g, 2 * half)
            if half == 1 and 0 < g < PASSES - 1:
                quantise_x(g + 1)
            if 0 < g < PASSES:
                make_h(g, 2 * half + 1)
            if is_tile(r + 3):
                normalise(r + 3)
            if is_tile(r + 4):
                invert_degree(r + 4)
            if half == 1 and 0 < g - 1 < PASSES:
                quantise_h(g - 1)
            if not turn_first and is_tile(r + 2):
                turn_adj(r + 2)
            if is_tile(r + 7) and on_tensor(r + 7):
                fold_rows(r + 7)
            if is_tile(r + 1):
                regroup_adj(r + 1)
